import numpy as np
import ml_dtypes


def mxq(x, axis, fmt="e4m3"):
    dtype, down = {"e4m3": (ml_dtypes.float8_e4m3fn, 7), "e5m2": (ml_dtypes.float8_e5m2, 14)}[fmt]
    v = np.moveaxis(np.asarray(x, np.float32).astype(ml_dtypes.bfloat16).astype(np.float64), axis, -1)
    blocks = v.reshape(v.shape[:-1] + (-1, 32))
    amax = np.abs(blocks).max(-1, keepdims=True)
    byte = np.maximum(np.where(amax > 0, np.frexp(amax)[1] - 1 + 127, 0) - down, 1)
    scale = np.exp2(byte - 127.0)
    codes = (blocks / scale).astype(np.float32).astype(dtype).astype(np.float64)
    return np.moveaxis((codes * scale).reshape(v.shape), -1, axis)


WIDE = False


def mx_kscale(k):
    if not WIDE:
        return np.ones(k)
    levels = np.array([10, -10, 5, -5, 0])
    a = np.random.permutation(np.resize(levels, k // 512 * 4)).reshape(k // 512, 4)
    idx = np.arange(k)
    return np.exp2(a[idx // 512, idx % 128 // 32])


BF16 = ml_dtypes.bfloat16


def bf(x):
    return np.asarray(x, np.float32).astype(BF16)


def f64(x):
    return np.asarray(x).astype(np.float64)


N, C, K, M, HH, WW, CO = 4, 512, 512, 128, 32, 32, 512
P = HH * WW


def setup_inputs():
    s, t = mx_kscale(K), mx_kscale(K)
    return {"h_pix": bf(np.maximum(np.random.standard_normal((N, K, P)), 0.0) * 1.5 * s[None, :, None]),
            "wp2": bf(np.random.standard_normal((K, K)) * np.sqrt(2.0 / K) * t[:, None] / s[None, :]),
            "sp2": bf(np.random.uniform(0.5, 1.5, K)),
            "bp2": bf(np.random.standard_normal(K) * 0.2 * t),
            "key_obj": bf(np.maximum(np.random.standard_normal((N, K, M)), 0.0) * 1.5 / t[None, :, None])}


def reference(h_pix, wp2, sp2, bp2, key_obj):
    y = mxq(f64(wp2), 1, "e4m3") @ mxq(f64(h_pix), 1, "e4m3")
    query = np.maximum(y * f64(sp2)[None, :, None] + f64(bp2)[None, :, None], 0.0)
    sim = (mxq(query, 1, "e4m3").transpose(0, 2, 1) @ mxq(f64(key_obj), 1, "e4m3")) * (K ** -0.5)
    e = np.exp(sim - sim.max(-1, keepdims=True))
    return e / e.sum(-1, keepdims=True)

@@ -1,0 +1,225 @@
+import math
+from contextlib import ExitStack
+
+import concourse.mybir as mybir
+from concourse.masks import make_identity
+
+F32 = mybir.dt.float32
+BF16 = mybir.dt.bfloat16
+U32 = mybir.dt.uint32
+U8 = mybir.dt.uint8
+FP8X4 = mybir.dt.float8_e4m3fn_x4
+ACT = mybir.ActivationFunctionType
+ALU = mybir.AluOpType
+
+P = 128
+PACK = 4
+IMAGES = 4
+CHANNELS = P * PACK
+PIXELS = 1024
+REGIONS = 128
+CHUNK = 512
+CHUNKS_PER_IMAGE = PIXELS // CHUNK
+CHUNKS = IMAGES * CHUNKS_PER_IMAGE
+PIXEL_TILES = CHUNK // P
+RUN = 4
+SIM_SCALE = 1.0 / math.sqrt(CHANNELS)
+
+FLOPS = 2 * IMAGES * PIXELS * CHANNELS * (CHANNELS + REGIONS)
+
+
+def tile_spatialocr_module_pa_kernel(tc, h_pix, wp2, sp2, bp2, key_obj, out):
+    nc = tc.nc
+    with ExitStack() as ctx:
+        ctx.enter_context(tc.manual_schedule())
+        once = ctx.enter_context(tc.tile_pool(name="once", bufs=1))
+        raw = ctx.enter_context(tc.tile_pool(name="raw", bufs=CHUNKS))
+        work = ctx.enter_context(tc.tile_pool(name="work", bufs=3))
+        small = ctx.enter_context(tc.tile_pool(name="small", bufs=4))
+        psum_y = ctx.enter_context(tc.psum_pool(name="psum_y", bufs=6))
+        psum_sim = ctx.enter_context(tc.psum_pool(name="psum_sim", bufs=2))
+
+        def interleave(grouped, planes):
+            nc.vector.tensor_copy(
+                out=grouped.rearrange("p (c i) t -> p c t i", i=RUN),
+                in_=planes.rearrange("p t (c i) -> p c t i", i=RUN),
+            )
+
+        def quantise(grouped, codes, scales):
+            nc.vector.quantize_mx(
+                out=codes.bitcast(FP8X4),
+                scales=scales,
+                in_=grouped.rearrange("p w t -> p (w t)"),
+            )
+
+        zero = once.tile([P, 1], F32)
+        one = once.tile([P, 1], F32)
+        nc.vector.memset(zero[:], 0.0)
+        nc.scalar.activation(out=one[:], in_=zero[:], func=ACT.Exp)
+
+        gain_bf = once.tile([P, PACK], BF16)
+        shift_bf = once.tile([P, PACK], BF16)
+        nc.scalar.dma_start(out=gain_bf[:], in_=sp2.rearrange("(p t) -> p t", t=PACK))
+        nc.scalar.dma_start(out=shift_bf[:], in_=bp2.rearrange("(p t) -> p t", t=PACK))
+
+        w_raw = once.tile([P, PACK * CHANNELS], BF16)
+        nc.sync.dma_start(out=w_raw[:], in_=wp2.rearrange("(m t) k -> m (t k)", t=PACK))
+
+        key_raw = once.tile([P, IMAGES, PACK, REGIONS], BF16)
+        h_raw = {}
+
+        def load_pixels(c):
+            n, half = divmod(c, CHUNKS_PER_IMAGE)
+            h_raw[c] = raw.tile([P, PACK, CHUNK], BF16, name="h_raw")
+            nc.sync.dma_start(
+                out=h_raw[c][:],
+                in_=h_pix[n, :, half * CHUNK : (half + 1) * CHUNK].rearrange(
+                    "(p t) w -> p t w", t=PACK
+                ),
+            )
+
+        load_pixels(0)
+        nc.sync.dma_start(out=key_raw[:], in_=key_obj.rearrange("n (p t) r -> p n t r", t=PACK))
+        for c in range(1, CHUNKS):
+            load_pixels(c)
+
+        identity = once.tile([P, P], F32)
+        make_identity(nc, identity[:])
+        gain = once.tile([P, PACK], F32)
+        shift = once.tile([P, PACK], F32)
+        nc.gpsimd.tensor_copy(out=gain[:], in_=gain_bf[:])
+        nc.gpsimd.tensor_copy(out=shift[:], in_=shift_bf[:])
+
+        w_words = w_raw[:].bitcast(F32).rearrange("m (t p u) -> m t u p", t=PACK, u=2)
+        w_grouped = once.tile([P, PACK * P * PACK], BF16, align_bytes=64)
+        w_grouped_words = w_grouped[:].bitcast(F32).rearrange("p (t m u) -> p t m u", t=PACK, u=2)
+        for pair in range(PACK // 2):
+            w_t = psum_y.tile([P, 2, 2, P], F32, tag="y")
+            for t in range(2):
+                for u in range(2):
+                    nc.tensor.transpose(w_t[:, t, u, :], w_words[:, 2 * pair + t, u, :], identity[:])
+            nc.scalar.copy(
+                out=w_grouped_words[:, 2 * pair : 2 * pair + 2, :, :],
+                in_=w_t[:].rearrange("p t u m -> p t m u"),
+            )
+        w_codes = once.tile([P, PACK * P], U32, align_bytes=64)
+        w_scales = once.tile([P, PACK * P], U8, align_bytes=64)
+
+        h_grouped, h_codes, h_scales = {}, {}, {}
+        q_planes, q_grouped, q_codes, q_scales = {}, {}, {}, {}
+        sim, shift_exp, row_sum, prob = {}, {}, {}, {}
+
+        def interleave_pixels(c):
+            h_grouped[c] = work.tile([P, CHUNK, PACK], BF16, name="h_grouped", align_bytes=64)
+            interleave(h_grouped[c][:], h_raw[c][:])
+
+        def quantise_pixels(c):
+            h_codes[c] = work.tile([P, CHUNK], U32, name="h_codes", align_bytes=64)
+            h_scales[c] = work.tile([P, CHUNK], U8, name="h_scales", align_bytes=64)
+            quantise(h_grouped[c][:], h_codes[c][:], h_scales[c][:])
+
+        def project(c):
+            q_planes[c] = work.tile([P, PACK, CHUNK], BF16, name="q_planes")
+            for t in range(PACK):
+                y = psum_y.tile([P, CHUNK], F32, tag="y")
+                nc.tensor.matmul_mx(
+                    out=y[:],
+                    lhsT=w_codes[:, t * P : (t + 1) * P].bitcast(FP8X4),
+                    lhsT_scale=w_scales[:, t * P : (t + 1) * P],
+                    rhs=h_codes[c][:].bitcast(FP8X4),
+                    rhs_scale=h_scales[c][:],
+                    start=True,
+                    stop=True,
+                )
+                nc.scalar.activation(
+                    out=q_planes[c][:, t, :],
+                    in_=y[:],
+                    func=ACT.Relu,
+                    bias=shift[:, t : t + 1],
+                    scale=gain[:, t : t + 1],
+                )
+
+        def interleave_query(c):
+            q_grouped[c] = work.tile([P, CHUNK, PACK], BF16, name="q_grouped", align_bytes=64)
+            interleave(q_grouped[c][:], q_planes[c][:])
+
+        def quantise_query(c):
+            q_codes[c] = work.tile([P, CHUNK], U32, name="q_codes", align_bytes=64)
+            q_scales[c] = work.tile([P, CHUNK], U8, name="q_scales", align_bytes=64)
+            quantise(q_grouped[c][:], q_codes[c][:], q_scales[c][:])
+
+        def attend(c):
+            n = c // CHUNKS_PER_IMAGE
+            sim[c] = psum_sim.tile([P, PIXEL_TILES, REGIONS], F32, name="sim")
+            for g in range(PIXEL_TILES):
+                nc.tensor.matmul_mx(
+                    out=sim[c][:, g, :],
+                    lhsT=q_codes[c][:, g * P : (g + 1) * P].bitcast(FP8X4),
+                    lhsT_scale=q_scales[c][:, g * P : (g + 1) * P],
+                    rhs=key_codes[:, n * REGIONS : (n + 1) * REGIONS].bitcast(FP8X4),
+                    rhs_scale=key_scales[:, n * REGIONS : (n + 1) * REGIONS],
+                    start=True,
+                    stop=True,
+                )
+
+        def exponentials(c):
+            row_max = small.tile([P, PIXEL_TILES], F32, name="row_max")
+            nc.vector.tensor_reduce(out=row_max[:], in_=sim[c][:], axis=mybir.AxisListType.X, op=ALU.max)
+            shift_exp[c] = small.tile([P, PIXEL_TILES], F32, name="shift_exp")
+            nc.vector.tensor_scalar_mul(out=shift_exp[c][:], in0=row_max[:], scalar1=-SIM_SCALE)
+            prob[c] = work.tile([P, PIXEL_TILES, REGIONS], F32, name="prob", bufs=4)
+            row_sum[c] = small.tile([P, PIXEL_TILES], F32, name="row_sum")
+            for g in range(PIXEL_TILES):
+                nc.scalar.activation(
+                    out=prob[c][:, g, :],
+                    in_=sim[c][:, g, :],
+                    func=ACT.Exp,
+                    bias=shift_exp[c][:, g : g + 1],
+                    scale=SIM_SCALE,
+                    accum_out=row_sum[c][:, g : g + 1],
+                )
+
+        def normalise_and_store(c):
+            n, half = divmod(c, CHUNKS_PER_IMAGE)
+            inverse = small.tile([P, PIXEL_TILES], F32, name="inverse")
+            nc.vector.reciprocal(out=inverse[:], in_=row_sum[c][:])
+            nc.vector.tensor_tensor(
+                out=prob[c][:],
+                in0=prob[c][:],
+                in1=inverse[:].unsqueeze(2).to_broadcast([P, PIXEL_TILES, REGIONS]),
+                op=ALU.mult,
+            )
+            nc.sync.dma_start(
+                out=out[n, half * CHUNK : (half + 1) * CHUNK, :].rearrange("(g p) r -> p g r", p=P),
+                in_=prob[c][:],
+            )
+
+        interleave_pixels(0)
+        quantise_pixels(0)
+        quantise(w_grouped[:].rearrange("p (w t) -> p w t", t=PACK), w_codes[:], w_scales[:])
+        key_grouped = once.tile([P, IMAGES * REGIONS, PACK], BF16, align_bytes=64)
+        key_codes = once.tile([P, IMAGES * REGIONS], U32, align_bytes=64)
+        key_scales = once.tile([P, IMAGES * REGIONS], U8, align_bytes=64)
+        for n in range(IMAGES):
+            interleave(key_grouped[:, n * REGIONS : (n + 1) * REGIONS, :], key_raw[:, n, :, :])
+        quantise(key_grouped[:], key_codes[:], key_scales[:])
+
+        def live(c):
+            return 0 <= c < CHUNKS
+
+        for i in range(CHUNKS + 3):
+            if live(i):
+                project(i)
+            if live(i - 2):
+                exponentials(i - 2)
+            if live(i + 1):
+                interleave_pixels(i + 1)
+            if live(i - 1):
+                interleave_query(i - 1)
+            if live(i - 3):
+                normalise_and_store(i - 3)
+            if live(i - 1):
+                quantise_query(i - 1)
+                attend(i - 1)
+            if live(i + 1):
+                quantise_pixels(i + 1)

@@ -31,7 +31,6 @@ FLOPS = 2 * IMAGES * PIXELS * CHANNELS * (CHANNELS + REGIONS)
 def tile_spatialocr_module_pa_kernel(tc, h_pix, wp2, sp2, bp2, key_obj, out):
     nc = tc.nc
     with ExitStack() as ctx:
-        ctx.enter_context(tc.manual_schedule())
         once = ctx.enter_context(tc.tile_pool(name="once", bufs=1))
         raw = ctx.enter_context(tc.tile_pool(name="raw", bufs=CHUNKS))
         work = ctx.enter_context(tc.tile_pool(name="work", bufs=3))

@@ -23,6 +23,7 @@ CHUNKS_PER_IMAGE = PIXELS // CHUNK
 CHUNKS = IMAGES * CHUNKS_PER_IMAGE
 PIXEL_TILES = CHUNK // P
 RUN = 4
+SCALAR_TILES = 3
 SIM_SCALE = 1.0 / math.sqrt(CHANNELS)
 
 FLOPS = 2 * IMAGES * PIXELS * CHANNELS * (CHANNELS + REGIONS)
@@ -38,8 +39,8 @@ def tile_spatialocr_module_pa_kernel(tc, h_pix, wp2, sp2, bp2, key_obj, out):
         psum_y = ctx.enter_context(tc.psum_pool(name="psum_y", bufs=6))
         psum_sim = ctx.enter_context(tc.psum_pool(name="psum_sim", bufs=2))
 
-        def interleave(grouped, planes):
-            nc.vector.tensor_copy(
+        def interleave(copy, grouped, planes):
+            copy(
                 out=grouped.rearrange("p (c i) t -> p c t i", i=RUN),
                 in_=planes.rearrange("p t (c i) -> p c t i", i=RUN),
             )
@@ -110,7 +111,7 @@ def tile_spatialocr_module_pa_kernel(tc, h_pix, wp2, sp2, bp2, key_obj, out):
 
         def interleave_pixels(c):
             h_grouped[c] = work.tile([P, CHUNK, PACK], BF16, name="h_grouped", align_bytes=64)
-            interleave(h_grouped[c][:], h_raw[c][:])
+            interleave(nc.vector.tensor_copy, h_grouped[c][:], h_raw[c][:])
 
         def quantise_pixels(c):
             h_codes[c] = work.tile([P, CHUNK], U32, name="h_codes", align_bytes=64)
@@ -140,7 +141,7 @@ def tile_spatialocr_module_pa_kernel(tc, h_pix, wp2, sp2, bp2, key_obj, out):
 
         def interleave_query(c):
             q_grouped[c] = work.tile([P, CHUNK, PACK], BF16, name="q_grouped", align_bytes=64)
-            interleave(q_grouped[c][:], q_planes[c][:])
+            interleave(nc.vector.tensor_copy, q_grouped[c][:], q_planes[c][:])
 
         def quantise_query(c):
             q_codes[c] = work.tile([P, CHUNK], U32, name="q_codes", align_bytes=64)
@@ -182,10 +183,19 @@ def tile_spatialocr_module_pa_kernel(tc, h_pix, wp2, sp2, bp2, key_obj, out):
             n, half = divmod(c, CHUNKS_PER_IMAGE)
             inverse = small.tile([P, PIXEL_TILES], F32, name="inverse")
             nc.vector.reciprocal(out=inverse[:], in_=row_sum[c][:])
+            for g in range(SCALAR_TILES):
+                nc.scalar.activation(
+                    out=prob[c][:, g, :],
+                    in_=prob[c][:, g, :],
+                    func=ACT.Copy,
+                    scale=inverse[:, g : g + 1],
+                )
             nc.vector.tensor_tensor(
-                out=prob[c][:],
-                in0=prob[c][:],
-                in1=inverse[:].unsqueeze(2).to_broadcast([P, PIXEL_TILES, REGIONS]),
+                out=prob[c][:, SCALAR_TILES:, :],
+                in0=prob[c][:, SCALAR_TILES:, :],
+                in1=inverse[:, SCALAR_TILES:]
+                .unsqueeze(2)
+                .to_broadcast([P, PIXEL_TILES - SCALAR_TILES, REGIONS]),
                 op=ALU.mult,
             )
             nc.sync.dma_start(
@@ -200,7 +210,9 @@ def tile_spatialocr_module_pa_kernel(tc, h_pix, wp2, sp2, bp2, key_obj, out):
         key_codes = once.tile([P, IMAGES * REGIONS], U32, align_bytes=64)
         key_scales = once.tile([P, IMAGES * REGIONS], U8, align_bytes=64)
         for n in range(IMAGES):
-            interleave(key_grouped[:, n * REGIONS : (n + 1) * REGIONS, :], key_raw[:, n, :, :])
+            interleave(
+                nc.scalar.copy, key_grouped[:, n * REGIONS : (n + 1) * REGIONS, :], key_raw[:, n, :, :]
+            )
         quantise(key_grouped[:], key_codes[:], key_scales[:])
 
         def live(c):

@@ -25,6 +25,10 @@ PIXEL_TILES = CHUNK // P
 RUN = 4
 SCALAR_TILES = 3
 SIM_SCALE = 1.0 / math.sqrt(CHANNELS)
+PIXELS_AHEAD = 2
+QUERY_BEHIND = 1
+SOFTMAX_BEHIND = 2
+STORE_BEHIND = 4
 
 FLOPS = 2 * IMAGES * PIXELS * CHANNELS * (CHANNELS + REGIONS)
 
@@ -34,8 +38,8 @@ def tile_spatialocr_module_pa_kernel(tc, h_pix, wp2, sp2, bp2, key_obj, out):
     with ExitStack() as ctx:
         once = ctx.enter_context(tc.tile_pool(name="once", bufs=1))
         raw = ctx.enter_context(tc.tile_pool(name="raw", bufs=CHUNKS))
-        work = ctx.enter_context(tc.tile_pool(name="work", bufs=3))
-        small = ctx.enter_context(tc.tile_pool(name="small", bufs=4))
+        work = ctx.enter_context(tc.tile_pool(name="work", bufs=4))
+        small = ctx.enter_context(tc.tile_pool(name="small", bufs=6))
         psum_y = ctx.enter_context(tc.psum_pool(name="psum_y", bufs=6))
         psum_sim = ctx.enter_context(tc.psum_pool(name="psum_sim", bufs=2))
 
@@ -107,7 +111,7 @@ def tile_spatialocr_module_pa_kernel(tc, h_pix, wp2, sp2, bp2, key_obj, out):
 
         h_grouped, h_codes, h_scales = {}, {}, {}
         q_planes, q_grouped, q_codes, q_scales = {}, {}, {}, {}
-        sim, shift_exp, row_sum, prob = {}, {}, {}, {}
+        sim, row_max, row_sum, inverse, prob = {}, {}, {}, {}, {}
 
         def interleave_pixels(c):
             h_grouped[c] = work.tile([P, CHUNK, PACK], BF16, name="h_grouped", align_bytes=64)
@@ -162,38 +166,44 @@ def tile_spatialocr_module_pa_kernel(tc, h_pix, wp2, sp2, bp2, key_obj, out):
                     stop=True,
                 )
 
+        def row_maxima(c):
+            row_max[c] = small.tile([P, PIXEL_TILES], F32, name="row_max")
+            nc.vector.tensor_reduce(
+                out=row_max[c][:], in_=sim[c][:], axis=mybir.AxisListType.X, op=ALU.max
+            )
+
         def exponentials(c):
-            row_max = small.tile([P, PIXEL_TILES], F32, name="row_max")
-            nc.vector.tensor_reduce(out=row_max[:], in_=sim[c][:], axis=mybir.AxisListType.X, op=ALU.max)
-            shift_exp[c] = small.tile([P, PIXEL_TILES], F32, name="shift_exp")
-            nc.vector.tensor_scalar_mul(out=shift_exp[c][:], in0=row_max[:], scalar1=-SIM_SCALE)
-            prob[c] = work.tile([P, PIXEL_TILES, REGIONS], F32, name="prob", bufs=4)
+            shift_exp = small.tile([P, PIXEL_TILES], F32, name="shift_exp")
+            nc.vector.tensor_scalar_mul(out=shift_exp[:], in0=row_max[c][:], scalar1=-SIM_SCALE)
+            prob[c] = work.tile([P, PIXEL_TILES, REGIONS], F32, name="prob", bufs=6)
             row_sum[c] = small.tile([P, PIXEL_TILES], F32, name="row_sum")
             for g in range(PIXEL_TILES):
                 nc.scalar.activation(
                     out=prob[c][:, g, :],
                     in_=sim[c][:, g, :],
                     func=ACT.Exp,
-                    bias=shift_exp[c][:, g : g + 1],
+                    bias=shift_exp[:, g : g + 1],
                     scale=SIM_SCALE,
                     accum_out=row_sum[c][:, g : g + 1],
                 )
 
+        def invert_row_sums(c):
+            inverse[c] = small.tile([P, PIXEL_TILES], F32, name="inverse")
+            nc.vector.reciprocal(out=inverse[c][:], in_=row_sum[c][:])
+
         def normalise_and_store(c):
             n, half = divmod(c, CHUNKS_PER_IMAGE)
-            inverse = small.tile([P, PIXEL_TILES], F32, name="inverse")
-            nc.vector.reciprocal(out=inverse[:], in_=row_sum[c][:])
             for g in range(SCALAR_TILES):
                 nc.scalar.activation(
                     out=prob[c][:, g, :],
                     in_=prob[c][:, g, :],
                     func=ACT.Copy,
-                    scale=inverse[:, g : g + 1],
+                    scale=inverse[c][:, g : g + 1],
                 )
             nc.vector.tensor_tensor(
                 out=prob[c][:, SCALAR_TILES:, :],
                 in0=prob[c][:, SCALAR_TILES:, :],
-                in1=inverse[:, SCALAR_TILES:]
+                in1=inverse[c][:, SCALAR_TILES:]
                 .unsqueeze(2)
                 .to_broadcast([P, PIXEL_TILES - SCALAR_TILES, REGIONS]),
                 op=ALU.mult,
@@ -214,23 +224,30 @@ def tile_spatialocr_module_pa_kernel(tc, h_pix, wp2, sp2, bp2, key_obj, out):
                 nc.scalar.copy, key_grouped[:, n * REGIONS : (n + 1) * REGIONS, :], key_raw[:, n, :, :]
             )
         quantise(key_grouped[:], key_codes[:], key_scales[:])
+        for c in range(1, PIXELS_AHEAD):
+            interleave_pixels(c)
+            quantise_pixels(c)
 
         def live(c):
             return 0 <= c < CHUNKS
 
-        for i in range(CHUNKS + 3):
+        for i in range(CHUNKS + STORE_BEHIND):
             if live(i):
                 project(i)
-            if live(i - 2):
-                exponentials(i - 2)
-            if live(i + 1):
-                interleave_pixels(i + 1)
-            if live(i - 1):
-                interleave_query(i - 1)
-            if live(i - 3):
-                normalise_and_store(i - 3)
-            if live(i - 1):
-                quantise_query(i - 1)
-                attend(i - 1)
-            if live(i + 1):
-                quantise_pixels(i + 1)
+            if live(i - SOFTMAX_BEHIND):
+                row_maxima(i - SOFTMAX_BEHIND)
+            if live(i + PIXELS_AHEAD):
+                interleave_pixels(i + PIXELS_AHEAD)
+            if live(i - SOFTMAX_BEHIND):
+                exponentials(i - SOFTMAX_BEHIND)
+            if live(i - STORE_BEHIND):
+                invert_row_sums(i - STORE_BEHIND)
+            if live(i - QUERY_BEHIND):
+                interleave_query(i - QUERY_BEHIND)
+            if live(i - STORE_BEHIND):
+                normalise_and_store(i - STORE_BEHIND)
+            if live(i - QUERY_BEHIND):
+                quantise_query(i - QUERY_BEHIND)
+                attend(i - QUERY_BEHIND)
+            if live(i + PIXELS_AHEAD):
+                quantise_pixels(i + PIXELS_AHEAD)

@@ -25,10 +25,6 @@ PIXEL_TILES = CHUNK // P
 RUN = 4
 SCALAR_TILES = 3
 SIM_SCALE = 1.0 / math.sqrt(CHANNELS)
-PIXELS_AHEAD = 2
-QUERY_BEHIND = 1
-SOFTMAX_BEHIND = 2
-STORE_BEHIND = 4
 
 FLOPS = 2 * IMAGES * PIXELS * CHANNELS * (CHANNELS + REGIONS)
 
@@ -38,8 +34,9 @@ def tile_spatialocr_module_pa_kernel(tc, h_pix, wp2, sp2, bp2, key_obj, out):
     with ExitStack() as ctx:
         once = ctx.enter_context(tc.tile_pool(name="once", bufs=1))
         raw = ctx.enter_context(tc.tile_pool(name="raw", bufs=CHUNKS))
-        work = ctx.enter_context(tc.tile_pool(name="work", bufs=4))
-        small = ctx.enter_context(tc.tile_pool(name="small", bufs=6))
+        blocks = ctx.enter_context(tc.tile_pool(name="blocks", bufs=PACK))
+        work = ctx.enter_context(tc.tile_pool(name="work", bufs=3))
+        small = ctx.enter_context(tc.tile_pool(name="small", bufs=4))
         psum_y = ctx.enter_context(tc.psum_pool(name="psum_y", bufs=6))
         psum_sim = ctx.enter_context(tc.psum_pool(name="psum_sim", bufs=2))
 
@@ -66,11 +63,7 @@ def tile_spatialocr_module_pa_kernel(tc, h_pix, wp2, sp2, bp2, key_obj, out):
         nc.scalar.dma_start(out=gain_bf[:], in_=sp2.rearrange("(p t) -> p t", t=PACK))
         nc.scalar.dma_start(out=shift_bf[:], in_=bp2.rearrange("(p t) -> p t", t=PACK))
 
-        w_raw = once.tile([P, PACK * CHANNELS], BF16)
-        nc.sync.dma_start(out=w_raw[:], in_=wp2.rearrange("(m t) k -> m (t k)", t=PACK))
-
-        key_raw = once.tile([P, IMAGES, PACK, REGIONS], BF16)
-        h_raw = {}
+        h_raw, w_raw, key_raw = {}, {}, {}
 
         def load_pixels(c):
             n, half = divmod(c, CHUNKS_PER_IMAGE)
@@ -82,10 +75,19 @@ def tile_spatialocr_module_pa_kernel(tc, h_pix, wp2, sp2, bp2, key_obj, out):
                 ),
             )
 
+        def load_keys(n):
+            key_raw[n] = blocks.tile([P, PACK, REGIONS], BF16, name="key_raw")
+            nc.sync.dma_start(out=key_raw[n][:], in_=key_obj[n].rearrange("(p t) r -> p t r", t=PACK))
+
         load_pixels(0)
-        nc.sync.dma_start(out=key_raw[:], in_=key_obj.rearrange("n (p t) r -> p n t r", t=PACK))
+        for t in range(PACK):
+            w_raw[t] = blocks.tile([P, CHANNELS], BF16, name="w_raw")
+            nc.sync.dma_start(out=w_raw[t][:], in_=wp2.rearrange("(m t) k -> t m k", t=PACK)[t])
+        load_keys(0)
         for c in range(1, CHUNKS):
             load_pixels(c)
+            if c % CHUNKS_PER_IMAGE == 0:
+                load_keys(c // CHUNKS_PER_IMAGE)
 
         identity = once.tile([P, P], F32)
         make_identity(nc, identity[:])
@@ -94,24 +96,10 @@ def tile_spatialocr_module_pa_kernel(tc, h_pix, wp2, sp2, bp2, key_obj, out):
         nc.gpsimd.tensor_copy(out=gain[:], in_=gain_bf[:])
         nc.gpsimd.tensor_copy(out=shift[:], in_=shift_bf[:])
 
-        w_words = w_raw[:].bitcast(F32).rearrange("m (t p u) -> m t u p", t=PACK, u=2)
-        w_grouped = once.tile([P, PACK * P * PACK], BF16, align_bytes=64)
-        w_grouped_words = w_grouped[:].bitcast(F32).rearrange("p (t m u) -> p t m u", t=PACK, u=2)
-        for pair in range(PACK // 2):
-            w_t = psum_y.tile([P, 2, 2, P], F32, tag="y")
-            for t in range(2):
-                for u in range(2):
-                    nc.tensor.transpose(w_t[:, t, u, :], w_words[:, 2 * pair + t, u, :], identity[:])
-            nc.scalar.copy(
-                out=w_grouped_words[:, 2 * pair : 2 * pair + 2, :, :],
-                in_=w_t[:].rearrange("p t u m -> p t m u"),
-            )
-        w_codes = once.tile([P, PACK * P], U32, align_bytes=64)
-        w_scales = once.tile([P, PACK * P], U8, align_bytes=64)
-
         h_grouped, h_codes, h_scales = {}, {}, {}
         q_planes, q_grouped, q_codes, q_scales = {}, {}, {}, {}
-        sim, row_max, row_sum, inverse, prob = {}, {}, {}, {}, {}
+        key_codes, key_scales = {}, {}
+        sim, row_sum, prob = {}, {}, {}
 
         def interleave_pixels(c):
             h_grouped[c] = work.tile([P, CHUNK, PACK], BF16, name="h_grouped", align_bytes=64)
@@ -143,6 +131,13 @@ def tile_spatialocr_module_pa_kernel(tc, h_pix, wp2, sp2, bp2, key_obj, out):
                     scale=gain[:, t : t + 1],
                 )
 
+        def prepare_keys(n):
+            key_grouped = blocks.tile([P, REGIONS, PACK], BF16, name="key_grouped", align_bytes=64)
+            interleave(nc.scalar.copy, key_grouped[:], key_raw[n][:])
+            key_codes[n] = blocks.tile([P, REGIONS], U32, name="key_codes", align_bytes=64)
+            key_scales[n] = blocks.tile([P, REGIONS], U8, name="key_scales", align_bytes=64)
+            quantise(key_grouped[:], key_codes[n][:], key_scales[n][:])
+
         def interleave_query(c):
             q_grouped[c] = work.tile([P, CHUNK, PACK], BF16, name="q_grouped", align_bytes=64)
             interleave(nc.vector.tensor_copy, q_grouped[c][:], q_planes[c][:])
@@ -160,22 +155,18 @@ def tile_spatialocr_module_pa_kernel(tc, h_pix, wp2, sp2, bp2, key_obj, out):
                     out=sim[c][:, g, :],
                     lhsT=q_codes[c][:, g * P : (g + 1) * P].bitcast(FP8X4),
                     lhsT_scale=q_scales[c][:, g * P : (g + 1) * P],
-                    rhs=key_codes[:, n * REGIONS : (n + 1) * REGIONS].bitcast(FP8X4),
-                    rhs_scale=key_scales[:, n * REGIONS : (n + 1) * REGIONS],
+                    rhs=key_codes[n][:].bitcast(FP8X4),
+                    rhs_scale=key_scales[n][:],
                     start=True,
                     stop=True,
                 )
 
-        def row_maxima(c):
-            row_max[c] = small.tile([P, PIXEL_TILES], F32, name="row_max")
-            nc.vector.tensor_reduce(
-                out=row_max[c][:], in_=sim[c][:], axis=mybir.AxisListType.X, op=ALU.max
-            )
-
         def exponentials(c):
+            row_max = small.tile([P, PIXEL_TILES], F32, name="row_max")
+            nc.vector.tensor_reduce(out=row_max[:], in_=sim[c][:], axis=mybir.AxisListType.X, op=ALU.max)
             shift_exp = small.tile([P, PIXEL_TILES], F32, name="shift_exp")
-            nc.vector.tensor_scalar_mul(out=shift_exp[:], in0=row_max[c][:], scalar1=-SIM_SCALE)
-            prob[c] = work.tile([P, PIXEL_TILES, REGIONS], F32, name="prob", bufs=6)
+            nc.vector.tensor_scalar_mul(out=shift_exp[:], in0=row_max[:], scalar1=-SIM_SCALE)
+            prob[c] = work.tile([P, PIXEL_TILES, REGIONS], F32, name="prob", bufs=4)
             row_sum[c] = small.tile([P, PIXEL_TILES], F32, name="row_sum")
             for g in range(PIXEL_TILES):
                 nc.scalar.activation(
@@ -187,67 +178,62 @@ def tile_spatialocr_module_pa_kernel(tc, h_pix, wp2, sp2, bp2, key_obj, out):
                     accum_out=row_sum[c][:, g : g + 1],
                 )
 
-        def invert_row_sums(c):
-            inverse[c] = small.tile([P, PIXEL_TILES], F32, name="inverse")
-            nc.vector.reciprocal(out=inverse[c][:], in_=row_sum[c][:])
-
         def normalise_and_store(c):
             n, half = divmod(c, CHUNKS_PER_IMAGE)
-            for g in range(SCALAR_TILES):
-                nc.scalar.activation(
-                    out=prob[c][:, g, :],
-                    in_=prob[c][:, g, :],
-                    func=ACT.Copy,
-                    scale=inverse[c][:, g : g + 1],
-                )
-            nc.vector.tensor_tensor(
-                out=prob[c][:, SCALAR_TILES:, :],
-                in0=prob[c][:, SCALAR_TILES:, :],
-                in1=inverse[c][:, SCALAR_TILES:]
-                .unsqueeze(2)
-                .to_broadcast([P, PIXEL_TILES - SCALAR_TILES, REGIONS]),
-                op=ALU.mult,
-            )
-            nc.sync.dma_start(
-                out=out[n, half * CHUNK : (half + 1) * CHUNK, :].rearrange("(g p) r -> p g r", p=P),
-                in_=prob[c][:],
-            )
+            inverse = small.tile([P, PIXEL_TILES], F32, name="inverse")
+            nc.vector.reciprocal(out=inverse[:], in_=row_sum[c][:])
+            for g in range(PIXEL_TILES):
+                if g < SCALAR_TILES:
+                    nc.scalar.activation(
+                        out=prob[c][:, g, :],
+                        in_=prob[c][:, g, :],
+                        func=ACT.Copy,
+                        scale=inverse[:, g : g + 1],
+                    )
+                else:
+                    nc.vector.tensor_scalar_mul(
+                        out=prob[c][:, g, :], in0=prob[c][:, g, :], scalar1=inverse[:, g : g + 1]
+                    )
+                first = half * CHUNK + g * P
+                nc.sync.dma_start(out=out[n, first : first + P, :], in_=prob[c][:, g, :])
 
         interleave_pixels(0)
         quantise_pixels(0)
-        quantise(w_grouped[:].rearrange("p (w t) -> p w t", t=PACK), w_codes[:], w_scales[:])
-        key_grouped = once.tile([P, IMAGES * REGIONS, PACK], BF16, align_bytes=64)
-        key_codes = once.tile([P, IMAGES * REGIONS], U32, align_bytes=64)
-        key_scales = once.tile([P, IMAGES * REGIONS], U8, align_bytes=64)
-        for n in range(IMAGES):
-            interleave(
-                nc.scalar.copy, key_grouped[:, n * REGIONS : (n + 1) * REGIONS, :], key_raw[:, n, :, :]
+
+        w_codes = once.tile([P, PACK * P], U32, align_bytes=64)
+        w_scales = once.tile([P, PACK * P], U8, align_bytes=64)
+        for t in range(PACK):
+            w_words = w_raw[t][:].bitcast(F32).rearrange("m (p u) -> m u p", u=2)
+            w_t = psum_y.tile([P, 2, P], F32, tag="y")
+            for u in range(2):
+                nc.tensor.transpose(w_t[:, u, :], w_words[:, u, :], identity[:])
+            w_grouped = blocks.tile([P, P, PACK], BF16, name="w_grouped", align_bytes=64)
+            nc.scalar.copy(
+                out=w_grouped[:].rearrange("p m t -> p (m t)").bitcast(F32).rearrange(
+                    "p (m u) -> p m u", u=2
+                ),
+                in_=w_t[:].rearrange("p u m -> p m u"),
             )
-        quantise(key_grouped[:], key_codes[:], key_scales[:])
-        for c in range(1, PIXELS_AHEAD):
-            interleave_pixels(c)
-            quantise_pixels(c)
+            quantise(w_grouped[:], w_codes[:, t * P : (t + 1) * P], w_scales[:, t * P : (t + 1) * P])
 
         def live(c):
             return 0 <= c < CHUNKS
 
-        for i in range(CHUNKS + STORE_BEHIND):
+        for i in range(CHUNKS + 3):
             if live(i):
                 project(i)
-            if live(i - SOFTMAX_BEHIND):
-                row_maxima(i - SOFTMAX_BEHIND)
-            if live(i + PIXELS_AHEAD):
-                interleave_pixels(i + PIXELS_AHEAD)
-            if live(i - SOFTMAX_BEHIND):
-                exponentials(i - SOFTMAX_BEHIND)
-            if live(i - STORE_BEHIND):
-                invert_row_sums(i - STORE_BEHIND)
-            if live(i - QUERY_BEHIND):
-                interleave_query(i - QUERY_BEHIND)
-            if live(i - STORE_BEHIND):
-                normalise_and_store(i - STORE_BEHIND)
-            if live(i - QUERY_BEHIND):
-                quantise_query(i - QUERY_BEHIND)
-                attend(i - QUERY_BEHIND)
-            if live(i + PIXELS_AHEAD):
-                quantise_pixels(i + PIXELS_AHEAD)
+                if i % CHUNKS_PER_IMAGE == 0:
+                    prepare_keys(i // CHUNKS_PER_IMAGE)
+            if live(i - 2):
+                exponentials(i - 2)
+            if live(i + 1):
+                interleave_pixels(i + 1)
+            if live(i - 1):
+                interleave_query(i - 1)
+            if live(i - 3):
+                normalise_and_store(i - 3)
+            if live(i - 1):
+                quantise_query(i - 1)
+                attend(i - 1)
+            if live(i + 1):
+                quantise_pixels(i + 1)

@@ -19,11 +19,8 @@ CHANNELS = P * PACK
 PIXELS = 1024
 REGIONS = 128
 CHUNK = 512
-CHUNKS_PER_IMAGE = PIXELS // CHUNK
-CHUNKS = IMAGES * CHUNKS_PER_IMAGE
-PIXEL_TILES = CHUNK // P
+LAST_IMAGE_WIDTHS = (512, 256, 128, 128)
 RUN = 4
-SCALAR_TILES = 3
 SIM_SCALE = 1.0 / math.sqrt(CHANNELS)
 
 FLOPS = 2 * IMAGES * PIXELS * CHANNELS * (CHANNELS + REGIONS)
@@ -33,6 +30,14 @@ def tile_spatialocr_module_pa_kernel(tc, h_pix, wp2, sp2, bp2, key_obj, out):
     nc = tc.nc
     with ExitStack() as ctx:
         once = ctx.enter_context(tc.tile_pool(name="once", bufs=1))
+        chunks = []
+        for n in range(IMAGES):
+            widths = LAST_IMAGE_WIDTHS if n == IMAGES - 1 else (CHUNK,) * (PIXELS // CHUNK)
+            first = 0
+            for width in widths:
+                chunks.append((n, first, width))
+                first += width
+        CHUNKS = len(chunks)
         raw = ctx.enter_context(tc.tile_pool(name="raw", bufs=CHUNKS))
         blocks = ctx.enter_context(tc.tile_pool(name="blocks", bufs=PACK))
         work = ctx.enter_context(tc.tile_pool(name="work", bufs=3))
@@ -66,11 +71,11 @@ def tile_spatialocr_module_pa_kernel(tc, h_pix, wp2, sp2, bp2, key_obj, out):
         h_raw, w_raw, key_raw = {}, {}, {}
 
         def load_pixels(c):
-            n, half = divmod(c, CHUNKS_PER_IMAGE)
-            h_raw[c] = raw.tile([P, PACK, CHUNK], BF16, name="h_raw")
+            n, first, width = chunks[c]
+            h_raw[c] = raw.tile([P, PACK, width], BF16, name="h_raw")
             nc.sync.dma_start(
                 out=h_raw[c][:],
-                in_=h_pix[n, :, half * CHUNK : (half + 1) * CHUNK].rearrange(
+                in_=h_pix[n, :, first : first + width].rearrange(
                     "(p t) w -> p t w", t=PACK
                 ),
             )
@@ -86,8 +91,8 @@ def tile_spatialocr_module_pa_kernel(tc, h_pix, wp2, sp2, bp2, key_obj, out):
         load_keys(0)
         for c in range(1, CHUNKS):
             load_pixels(c)
-            if c % CHUNKS_PER_IMAGE == 0:
-                load_keys(c // CHUNKS_PER_IMAGE)
+            if chunks[c][1] == 0:
+                load_keys(chunks[c][0])
 
         identity = once.tile([P, P], F32)
         make_identity(nc, identity[:])
@@ -102,18 +107,18 @@ def tile_spatialocr_module_pa_kernel(tc, h_pix, wp2, sp2, bp2, key_obj, out):
         sim, row_sum, prob = {}, {}, {}
 
         def interleave_pixels(c):
-            h_grouped[c] = work.tile([P, CHUNK, PACK], BF16, name="h_grouped", align_bytes=64)
+            h_grouped[c] = work.tile([P, chunks[c][2], PACK], BF16, name="h_grouped", align_bytes=64)
             interleave(nc.vector.tensor_copy, h_grouped[c][:], h_raw[c][:])
 
         def quantise_pixels(c):
-            h_codes[c] = work.tile([P, CHUNK], U32, name="h_codes", align_bytes=64)
-            h_scales[c] = work.tile([P, CHUNK], U8, name="h_scales", align_bytes=64)
+            h_codes[c] = work.tile([P, chunks[c][2]], U32, name="h_codes", align_bytes=64)
+            h_scales[c] = work.tile([P, chunks[c][2]], U8, name="h_scales", align_bytes=64)
             quantise(h_grouped[c][:], h_codes[c][:], h_scales[c][:])
 
         def project(c):
-            q_planes[c] = work.tile([P, PACK, CHUNK], BF16, name="q_planes")
+            q_planes[c] = work.tile([P, PACK, chunks[c][2]], BF16, name="q_planes")
             for t in range(PACK):
-                y = psum_y.tile([P, CHUNK], F32, tag="y")
+                y = psum_y.tile([P, chunks[c][2]], F32, tag="y")
                 nc.tensor.matmul_mx(
                     out=y[:],
                     lhsT=w_codes[:, t * P : (t + 1) * P].bitcast(FP8X4),
@@ -139,18 +144,18 @@ def tile_spatialocr_module_pa_kernel(tc, h_pix, wp2, sp2, bp2, key_obj, out):
             quantise(key_grouped[:], key_codes[n][:], key_scales[n][:])
 
         def interleave_query(c):
-            q_grouped[c] = work.tile([P, CHUNK, PACK], BF16, name="q_grouped", align_bytes=64)
+            q_grouped[c] = work.tile([P, chunks[c][2], PACK], BF16, name="q_grouped", align_bytes=64)
             interleave(nc.vector.tensor_copy, q_grouped[c][:], q_planes[c][:])
 
         def quantise_query(c):
-            q_codes[c] = work.tile([P, CHUNK], U32, name="q_codes", align_bytes=64)
-            q_scales[c] = work.tile([P, CHUNK], U8, name="q_scales", align_bytes=64)
+            q_codes[c] = work.tile([P, chunks[c][2]], U32, name="q_codes", align_bytes=64)
+            q_scales[c] = work.tile([P, chunks[c][2]], U8, name="q_scales", align_bytes=64)
             quantise(q_grouped[c][:], q_codes[c][:], q_scales[c][:])
 
         def attend(c):
-            n = c // CHUNKS_PER_IMAGE
-            sim[c] = psum_sim.tile([P, PIXEL_TILES, REGIONS], F32, name="sim")
-            for g in range(PIXEL_TILES):
+            n = chunks[c][0]
+            sim[c] = psum_sim.tile([P, chunks[c][2] // P, REGIONS], F32, name="sim")
+            for g in range(chunks[c][2] // P):
                 nc.tensor.matmul_mx(
                     out=sim[c][:, g, :],
                     lhsT=q_codes[c][:, g * P : (g + 1) * P].bitcast(FP8X4),
@@ -162,13 +167,14 @@ def tile_spatialocr_module_pa_kernel(tc, h_pix, wp2, sp2, bp2, key_obj, out):
                 )
 
         def exponentials(c):
-            row_max = small.tile([P, PIXEL_TILES], F32, name="row_max")
+            tiles = chunks[c][2] // P
+            row_max = small.tile([P, tiles], F32, name="row_max")
             nc.vector.tensor_reduce(out=row_max[:], in_=sim[c][:], axis=mybir.AxisListType.X, op=ALU.max)
-            shift_exp = small.tile([P, PIXEL_TILES], F32, name="shift_exp")
+            shift_exp = small.tile([P, tiles], F32, name="shift_exp")
             nc.vector.tensor_scalar_mul(out=shift_exp[:], in0=row_max[:], scalar1=-SIM_SCALE)
-            prob[c] = work.tile([P, PIXEL_TILES, REGIONS], F32, name="prob", bufs=4)
-            row_sum[c] = small.tile([P, PIXEL_TILES], F32, name="row_sum")
-            for g in range(PIXEL_TILES):
+            prob[c] = work.tile([P, tiles, REGIONS], F32, name="prob", bufs=4)
+            row_sum[c] = small.tile([P, tiles], F32, name="row_sum")
+            for g in range(tiles):
                 nc.scalar.activation(
                     out=prob[c][:, g, :],
                     in_=sim[c][:, g, :],
@@ -179,11 +185,12 @@ def tile_spatialocr_module_pa_kernel(tc, h_pix, wp2, sp2, bp2, key_obj, out):
                 )
 
         def normalise_and_store(c):
-            n, half = divmod(c, CHUNKS_PER_IMAGE)
-            inverse = small.tile([P, PIXEL_TILES], F32, name="inverse")
+            n, start, width = chunks[c]
+            tiles = width // P
+            inverse = small.tile([P, tiles], F32, name="inverse")
             nc.vector.reciprocal(out=inverse[:], in_=row_sum[c][:])
-            for g in range(PIXEL_TILES):
-                if g < SCALAR_TILES:
+            for g in range(tiles):
+                if g < tiles - 1:
                     nc.scalar.activation(
                         out=prob[c][:, g, :],
                         in_=prob[c][:, g, :],
@@ -194,7 +201,7 @@ def tile_spatialocr_module_pa_kernel(tc, h_pix, wp2, sp2, bp2, key_obj, out):
                     nc.vector.tensor_scalar_mul(
                         out=prob[c][:, g, :], in0=prob[c][:, g, :], scalar1=inverse[:, g : g + 1]
                     )
-                first = half * CHUNK + g * P
+                first = start + g * P
                 nc.sync.dma_start(out=out[n, first : first + P, :], in_=prob[c][:, g, :])
 
         interleave_pixels(0)
@@ -222,8 +229,8 @@ def tile_spatialocr_module_pa_kernel(tc, h_pix, wp2, sp2, bp2, key_obj, out):
         for i in range(CHUNKS + 3):
             if live(i):
                 project(i)
-                if i % CHUNKS_PER_IMAGE == 0:
-                    prepare_keys(i // CHUNKS_PER_IMAGE)
+                if chunks[i][1] == 0:
+                    prepare_keys(chunks[i][0])
             if live(i - 2):
                 exponentials(i - 2)
             if live(i + 1):

@@ -20,6 +20,7 @@ PIXELS = 1024
 REGIONS = 128
 CHUNK = 512
 LAST_IMAGE_WIDTHS = (512, 256, 128, 128)
+SCALAR_SHARE = 64
 RUN = 4
 SIM_SCALE = 1.0 / math.sqrt(CHANNELS)
 
@@ -70,15 +71,20 @@ def tile_spatialocr_module_pa_kernel(tc, h_pix, wp2, sp2, bp2, key_obj, out):
 
         h_raw, w_raw, key_raw = {}, {}, {}
 
+        def pieces(c):
+            return 2 if c == 0 else 1
+
         def load_pixels(c):
             n, first, width = chunks[c]
             h_raw[c] = raw.tile([P, PACK, width], BF16, name="h_raw")
-            nc.sync.dma_start(
-                out=h_raw[c][:],
-                in_=h_pix[n, :, first : first + width].rearrange(
-                    "(p t) w -> p t w", t=PACK
-                ),
-            )
+            piece = width // pieces(c)
+            for lo in range(0, width, piece):
+                nc.sync.dma_start(
+                    out=h_raw[c][:, :, lo : lo + piece],
+                    in_=h_pix[n, :, first + lo : first + lo + piece].rearrange(
+                        "(p t) w -> p t w", t=PACK
+                    ),
+                )
 
         def load_keys(n):
             key_raw[n] = blocks.tile([P, PACK, REGIONS], BF16, name="key_raw")
@@ -108,7 +114,13 @@ def tile_spatialocr_module_pa_kernel(tc, h_pix, wp2, sp2, bp2, key_obj, out):
 
         def interleave_pixels(c):
             h_grouped[c] = work.tile([P, chunks[c][2], PACK], BF16, name="h_grouped", align_bytes=64)
-            interleave(nc.vector.tensor_copy, h_grouped[c][:], h_raw[c][:])
+            piece = chunks[c][2] // pieces(c)
+            for lo in range(0, chunks[c][2], piece):
+                interleave(
+                    nc.vector.tensor_copy,
+                    h_grouped[c][:, lo : lo + piece, :],
+                    h_raw[c][:, :, lo : lo + piece],
+                )
 
         def quantise_pixels(c):
             h_codes[c] = work.tile([P, chunks[c][2]], U32, name="h_codes", align_bytes=64)
@@ -145,7 +157,10 @@ def tile_spatialocr_module_pa_kernel(tc, h_pix, wp2, sp2, bp2, key_obj, out):
 
         def interleave_query(c):
             q_grouped[c] = work.tile([P, chunks[c][2], PACK], BF16, name="q_grouped", align_bytes=64)
-            interleave(nc.vector.tensor_copy, q_grouped[c][:], q_planes[c][:])
+            mine = chunks[c][2] - (SCALAR_SHARE if chunks[c][2] == CHUNK else 0)
+            interleave(nc.vector.tensor_copy, q_grouped[c][:, :mine, :], q_planes[c][:, :, :mine])
+            if mine < chunks[c][2]:
+                interleave(nc.scalar.copy, q_grouped[c][:, mine:, :], q_planes[c][:, :, mine:])
 
         def quantise_query(c):
             q_codes[c] = work.tile([P, chunks[c][2]], U32, name="q_codes", align_bytes=64)

@@ -20,7 +20,7 @@ PIXELS = 1024
 REGIONS = 128
 CHUNK = 512
 LAST_IMAGE_WIDTHS = (512, 256, 128, 128)
-SCALAR_SHARE = 64
+SCALAR_SHARE = 48
 RUN = 4
 SIM_SCALE = 1.0 / math.sqrt(CHANNELS)
 

@@ -41,8 +41,8 @@ def tile_spatialocr_module_pa_kernel(tc, h_pix, wp2, sp2, bp2, key_obj, out):
         CHUNKS = len(chunks)
         raw = ctx.enter_context(tc.tile_pool(name="raw", bufs=CHUNKS))
         blocks = ctx.enter_context(tc.tile_pool(name="blocks", bufs=PACK))
-        work = ctx.enter_context(tc.tile_pool(name="work", bufs=3))
-        small = ctx.enter_context(tc.tile_pool(name="small", bufs=4))
+        work = ctx.enter_context(tc.tile_pool(name="work", bufs=4))
+        small = ctx.enter_context(tc.tile_pool(name="small", bufs=6))
         psum_y = ctx.enter_context(tc.psum_pool(name="psum_y", bufs=6))
         psum_sim = ctx.enter_context(tc.psum_pool(name="psum_sim", bufs=2))
 
@@ -109,18 +109,23 @@ def tile_spatialocr_module_pa_kernel(tc, h_pix, wp2, sp2, bp2, key_obj, out):
 
         h_grouped, h_codes, h_scales = {}, {}, {}
         q_planes, q_grouped, q_codes, q_scales = {}, {}, {}, {}
-        key_codes, key_scales = {}, {}
-        sim, row_sum, prob = {}, {}, {}
+        key_grouped, key_codes, key_scales = {}, {}, {}
+        y_banks, sim, row_max, shift_exp, row_sum, inverse, prob = {}, {}, {}, {}, {}, {}, {}
 
-        def interleave_pixels(c):
+        def interleave_pixels(c, half):
+            if half == 0:
+                h_grouped[c] = work.tile([P, chunks[c][2], PACK], BF16, name="h_grouped", align_bytes=64)
+            piece = chunks[c][2] // 2
+            lo = half * piece
+            interleave(
+                nc.vector.tensor_copy,
+                h_grouped[c][:, lo : lo + piece, :],
+                h_raw[c][:, :, lo : lo + piece],
+            )
+
+        def whole_pixels(c):
             h_grouped[c] = work.tile([P, chunks[c][2], PACK], BF16, name="h_grouped", align_bytes=64)
-            piece = chunks[c][2] // pieces(c)
-            for lo in range(0, chunks[c][2], piece):
-                interleave(
-                    nc.vector.tensor_copy,
-                    h_grouped[c][:, lo : lo + piece, :],
-                    h_raw[c][:, :, lo : lo + piece],
-                )
+            interleave(nc.vector.tensor_copy, h_grouped[c][:], h_raw[c][:])
 
         def quantise_pixels(c):
             h_codes[c] = work.tile([P, chunks[c][2]], U32, name="h_codes", align_bytes=64)
@@ -128,9 +133,10 @@ def tile_spatialocr_module_pa_kernel(tc, h_pix, wp2, sp2, bp2, key_obj, out):
             quantise(h_grouped[c][:], h_codes[c][:], h_scales[c][:])
 
         def project(c):
-            q_planes[c] = work.tile([P, PACK, chunks[c][2]], BF16, name="q_planes")
+            y_banks[c] = []
             for t in range(PACK):
                 y = psum_y.tile([P, chunks[c][2]], F32, tag="y")
+                y_banks[c].append(y)
                 nc.tensor.matmul_mx(
                     out=y[:],
                     lhsT=w_codes[:, t * P : (t + 1) * P].bitcast(FP8X4),
@@ -140,27 +146,39 @@ def tile_spatialocr_module_pa_kernel(tc, h_pix, wp2, sp2, bp2, key_obj, out):
                     start=True,
                     stop=True,
                 )
+
+        def rectify(c):
+            q_planes[c] = work.tile([P, PACK, chunks[c][2]], BF16, name="q_planes")
+            for t in range(PACK):
                 nc.scalar.activation(
                     out=q_planes[c][:, t, :],
-                    in_=y[:],
+                    in_=y_banks[c][t][:],
                     func=ACT.Relu,
                     bias=shift[:, t : t + 1],
                     scale=gain[:, t : t + 1],
                 )
 
-        def prepare_keys(n):
-            key_grouped = blocks.tile([P, REGIONS, PACK], BF16, name="key_grouped", align_bytes=64)
-            interleave(nc.scalar.copy, key_grouped[:], key_raw[n][:])
+        def interleave_keys(n):
+            key_grouped[n] = blocks.tile([P, REGIONS, PACK], BF16, name="key_grouped", align_bytes=64)
+            interleave(nc.scalar.copy, key_grouped[n][:], key_raw[n][:])
+
+        def quantise_keys(n):
             key_codes[n] = blocks.tile([P, REGIONS], U32, name="key_codes", align_bytes=64)
             key_scales[n] = blocks.tile([P, REGIONS], U8, name="key_scales", align_bytes=64)
-            quantise(key_grouped[:], key_codes[n][:], key_scales[n][:])
+            quantise(key_grouped[n][:], key_codes[n][:], key_scales[n][:])
 
-        def interleave_query(c):
+        def vector_share(c):
+            return chunks[c][2] - (SCALAR_SHARE if chunks[c][2] == CHUNK else 0)
+
+        def interleave_query_on_scalar(c):
             q_grouped[c] = work.tile([P, chunks[c][2], PACK], BF16, name="q_grouped", align_bytes=64)
-            mine = chunks[c][2] - (SCALAR_SHARE if chunks[c][2] == CHUNK else 0)
-            interleave(nc.vector.tensor_copy, q_grouped[c][:, :mine, :], q_planes[c][:, :, :mine])
+            mine = vector_share(c)
             if mine < chunks[c][2]:
                 interleave(nc.scalar.copy, q_grouped[c][:, mine:, :], q_planes[c][:, :, mine:])
+
+        def interleave_query_on_vector(c):
+            mine = vector_share(c)
+            interleave(nc.vector.tensor_copy, q_grouped[c][:, :mine, :], q_planes[c][:, :, :mine])
 
         def quantise_query(c):
             q_codes[c] = work.tile([P, chunks[c][2]], U32, name="q_codes", align_bytes=64)
@@ -181,12 +199,16 @@ def tile_spatialocr_module_pa_kernel(tc, h_pix, wp2, sp2, bp2, key_obj, out):
                     stop=True,
                 )
 
+        def row_maxima(c):
+            row_max[c] = small.tile([P, chunks[c][2] // P], F32, name="row_max")
+            nc.vector.tensor_reduce(out=row_max[c][:], in_=sim[c][:], axis=mybir.AxisListType.X, op=ALU.max)
+
+        def scale_maxima(c):
+            shift_exp[c] = small.tile([P, chunks[c][2] // P], F32, name="shift_exp")
+            nc.vector.tensor_scalar_mul(out=shift_exp[c][:], in0=row_max[c][:], scalar1=-SIM_SCALE)
+
         def exponentials(c):
             tiles = chunks[c][2] // P
-            row_max = small.tile([P, tiles], F32, name="row_max")
-            nc.vector.tensor_reduce(out=row_max[:], in_=sim[c][:], axis=mybir.AxisListType.X, op=ALU.max)
-            shift_exp = small.tile([P, tiles], F32, name="shift_exp")
-            nc.vector.tensor_scalar_mul(out=shift_exp[:], in0=row_max[:], scalar1=-SIM_SCALE)
             prob[c] = work.tile([P, tiles, REGIONS], F32, name="prob", bufs=4)
             row_sum[c] = small.tile([P, tiles], F32, name="row_sum")
             for g in range(tiles):
@@ -194,68 +216,97 @@ def tile_spatialocr_module_pa_kernel(tc, h_pix, wp2, sp2, bp2, key_obj, out):
                     out=prob[c][:, g, :],
                     in_=sim[c][:, g, :],
                     func=ACT.Exp,
-                    bias=shift_exp[:, g : g + 1],
+                    bias=shift_exp[c][:, g : g + 1],
                     scale=SIM_SCALE,
                     accum_out=row_sum[c][:, g : g + 1],
                 )
 
-        def normalise_and_store(c):
-            n, start, width = chunks[c]
-            tiles = width // P
-            inverse = small.tile([P, tiles], F32, name="inverse")
-            nc.vector.reciprocal(out=inverse[:], in_=row_sum[c][:])
-            for g in range(tiles):
-                if g < tiles - 1:
-                    nc.scalar.activation(
-                        out=prob[c][:, g, :],
-                        in_=prob[c][:, g, :],
-                        func=ACT.Copy,
-                        scale=inverse[:, g : g + 1],
-                    )
-                else:
-                    nc.vector.tensor_scalar_mul(
-                        out=prob[c][:, g, :], in0=prob[c][:, g, :], scalar1=inverse[:, g : g + 1]
-                    )
-                first = start + g * P
-                nc.sync.dma_start(out=out[n, first : first + P, :], in_=prob[c][:, g, :])
+        def invert_sums(c):
+            inverse[c] = small.tile([P, chunks[c][2] // P], F32, name="inverse")
+            nc.vector.reciprocal(out=inverse[c][:], in_=row_sum[c][:])
 
-        interleave_pixels(0)
-        quantise_pixels(0)
+        def normalise_on_vector(c):
+            g = chunks[c][2] // P - 1
+            nc.vector.tensor_scalar_mul(
+                out=prob[c][:, g, :], in0=prob[c][:, g, :], scalar1=inverse[c][:, g : g + 1]
+            )
+            store(c, g)
+
+        def normalise_on_scalar(c):
+            for g in range(chunks[c][2] // P - 1):
+                nc.scalar.activation(
+                    out=prob[c][:, g, :],
+                    in_=prob[c][:, g, :],
+                    func=ACT.Copy,
+                    scale=inverse[c][:, g : g + 1],
+                )
+                store(c, g)
+
+        def store(c, g):
+            n, start, width = chunks[c]
+            first = start + g * P
+            nc.sync.dma_start(out=out[n, first : first + P, :], in_=prob[c][:, g, :])
 
         w_codes = once.tile([P, PACK * P], U32, align_bytes=64)
         w_scales = once.tile([P, PACK * P], U8, align_bytes=64)
-        for t in range(PACK):
-            w_words = w_raw[t][:].bitcast(F32).rearrange("m (p u) -> m u p", u=2)
-            w_t = psum_y.tile([P, 2, P], F32, tag="y")
-            for u in range(2):
-                nc.tensor.transpose(w_t[:, u, :], w_words[:, u, :], identity[:])
-            w_grouped = blocks.tile([P, P, PACK], BF16, name="w_grouped", align_bytes=64)
-            nc.scalar.copy(
-                out=w_grouped[:].rearrange("p m t -> p (m t)").bitcast(F32).rearrange(
-                    "p (m u) -> p m u", u=2
-                ),
-                in_=w_t[:].rearrange("p u m -> p m u"),
-            )
-            quantise(w_grouped[:], w_codes[:, t * P : (t + 1) * P], w_scales[:, t * P : (t + 1) * P])
+
+        def prepare_weights():
+            for t in range(PACK):
+                w_words = w_raw[t][:].bitcast(F32).rearrange("m (p u) -> m u p", u=2)
+                w_t = psum_y.tile([P, 2, P], F32, tag="y")
+                for u in range(2):
+                    nc.tensor.transpose(w_t[:, u, :], w_words[:, u, :], identity[:])
+                w_grouped = blocks.tile([P, P, PACK], BF16, name="w_grouped", align_bytes=64)
+                nc.scalar.copy(
+                    out=w_grouped[:].rearrange("p m t -> p (m t)").bitcast(F32).rearrange(
+                        "p (m u) -> p m u", u=2
+                    ),
+                    in_=w_t[:].rearrange("p u m -> p m u"),
+                )
+                quantise(w_grouped[:], w_codes[:, t * P : (t + 1) * P], w_scales[:, t * P : (t + 1) * P])
 
         def live(c):
             return 0 <= c < CHUNKS
 
-        for i in range(CHUNKS + 3):
-            if live(i):
-                project(i)
-                if chunks[i][1] == 0:
-                    prepare_keys(chunks[i][0])
-            if live(i - 2):
-                exponentials(i - 2)
-            if live(i + 1):
-                interleave_pixels(i + 1)
-            if live(i - 1):
-                interleave_query(i - 1)
-            if live(i - 3):
-                normalise_and_store(i - 3)
-            if live(i - 1):
-                quantise_query(i - 1)
-                attend(i - 1)
-            if live(i + 1):
-                quantise_pixels(i + 1)
+        with tc.manual_schedule(engines={mybir.EngineType.Activation, mybir.EngineType.DVE, mybir.EngineType.PE}):
+            interleave_pixels(0, 0)
+            interleave_pixels(0, 1)
+            quantise_pixels(0)
+            prepare_weights()
+            interleave_keys(0)
+            project(0)
+            whole_pixels(1)
+            quantise_keys(0)
+            quantise_pixels(1)
+            for i in range(CHUNKS + 3):
+                if live(i - 3):
+                    exponentials(i - 3)
+                if live(i):
+                    rectify(i)
+                if live(i + 1):
+                    project(i + 1)
+                if live(i - 1):
+                    interleave_query_on_vector(i - 1)
+                if live(i + 2):
+                    whole_pixels(i + 2)
+                if live(i - 1):
+                    quantise_query(i - 1)
+                    attend(i - 1)
+                if live(i - 2):
+                    row_maxima(i - 2)
+                if live(i - 3):
+                    invert_sums(i - 3)
+                if live(i + 2):
+                    quantise_pixels(i + 2)
+                if live(i - 2):
+                    scale_maxima(i - 2)
+                if live(i - 3):
+                    normalise_on_vector(i - 3)
+                if live(i):
+                    interleave_query_on_scalar(i)
+                if live(i - 3):
+                    normalise_on_scalar(i - 3)
+                if live(i + 1) and i > 0 and chunks[i + 1][1] == 0:
+                    interleave_keys(chunks[i + 1][0])
+                if live(i) and i > 0 and chunks[i][1] == 0:
+                    quantise_keys(chunks[i][0])

@@ -19,8 +19,9 @@ CHANNELS = P * PACK
 PIXELS = 1024
 REGIONS = 128
 CHUNK = 512
-LAST_IMAGE_WIDTHS = (512, 256, 128, 128)
-SCALAR_SHARE = 48
+LAST_IMAGE_WIDTHS = (512, 256, 256)
+SCALAR_SHARE = 144
+VECTOR_TILES = 3
 RUN = 4
 SIM_SCALE = 1.0 / math.sqrt(CHANNELS)
 
@@ -42,7 +43,7 @@ def tile_spatialocr_module_pa_kernel(tc, h_pix, wp2, sp2, bp2, key_obj, out):
         raw = ctx.enter_context(tc.tile_pool(name="raw", bufs=CHUNKS))
         blocks = ctx.enter_context(tc.tile_pool(name="blocks", bufs=PACK))
         work = ctx.enter_context(tc.tile_pool(name="work", bufs=4))
-        small = ctx.enter_context(tc.tile_pool(name="small", bufs=6))
+        small = ctx.enter_context(tc.tile_pool(name="small", bufs=8))
         psum_y = ctx.enter_context(tc.psum_pool(name="psum_y", bufs=6))
         psum_sim = ctx.enter_context(tc.psum_pool(name="psum_sim", bufs=2))
 
@@ -205,7 +206,14 @@ def tile_spatialocr_module_pa_kernel(tc, h_pix, wp2, sp2, bp2, key_obj, out):
 
         def scale_maxima(c):
             shift_exp[c] = small.tile([P, chunks[c][2] // P], F32, name="shift_exp")
-            nc.vector.tensor_scalar_mul(out=shift_exp[c][:], in0=row_max[c][:], scalar1=-SIM_SCALE)
+            nc.gpsimd.tensor_scalar(
+                out=shift_exp[c][:],
+                in0=row_max[c][:],
+                scalar1=-SIM_SCALE,
+                scalar2=0.0,
+                op0=ALU.mult,
+                op1=ALU.add,
+            )
 
         def exponentials(c):
             tiles = chunks[c][2] // P
@@ -226,14 +234,15 @@ def tile_spatialocr_module_pa_kernel(tc, h_pix, wp2, sp2, bp2, key_obj, out):
             nc.vector.reciprocal(out=inverse[c][:], in_=row_sum[c][:])
 
         def normalise_on_vector(c):
-            g = chunks[c][2] // P - 1
-            nc.vector.tensor_scalar_mul(
-                out=prob[c][:, g, :], in0=prob[c][:, g, :], scalar1=inverse[c][:, g : g + 1]
-            )
-            store(c, g)
+            tiles = chunks[c][2] // P
+            for g in range(max(0, tiles - VECTOR_TILES), tiles):
+                nc.vector.tensor_scalar_mul(
+                    out=prob[c][:, g, :], in0=prob[c][:, g, :], scalar1=inverse[c][:, g : g + 1]
+                )
+                store(c, g)
 
         def normalise_on_scalar(c):
-            for g in range(chunks[c][2] // P - 1):
+            for g in range(chunks[c][2] // P - VECTOR_TILES):
                 nc.scalar.activation(
                     out=prob[c][:, g, :],
                     in_=prob[c][:, g, :],
@@ -268,7 +277,9 @@ def tile_spatialocr_module_pa_kernel(tc, h_pix, wp2, sp2, bp2, key_obj, out):
         def live(c):
             return 0 <= c < CHUNKS
 
-        with tc.manual_schedule(engines={mybir.EngineType.Activation, mybir.EngineType.DVE, mybir.EngineType.PE}):
+        with tc.manual_schedule(
+            engines={mybir.EngineType.Activation, mybir.EngineType.DVE, mybir.EngineType.PE}
+        ):
             interleave_pixels(0, 0)
             interleave_pixels(0, 1)
             quantise_pixels(0)
@@ -278,11 +289,11 @@ def tile_spatialocr_module_pa_kernel(tc, h_pix, wp2, sp2, bp2, key_obj, out):
             whole_pixels(1)
             quantise_keys(0)
             quantise_pixels(1)
-            for i in range(CHUNKS + 3):
-                if live(i - 3):
-                    exponentials(i - 3)
+            for i in range(CHUNKS + 4):
                 if live(i):
                     rectify(i)
+                if live(i - 3):
+                    exponentials(i - 3)
                 if live(i + 1):
                     project(i + 1)
                 if live(i - 1):
@@ -292,21 +303,21 @@ def tile_spatialocr_module_pa_kernel(tc, h_pix, wp2, sp2, bp2, key_obj, out):
                 if live(i - 1):
                     quantise_query(i - 1)
                     attend(i - 1)
+                if live(i - 4):
+                    invert_sums(i - 4)
                 if live(i - 2):
                     row_maxima(i - 2)
-                if live(i - 3):
-                    invert_sums(i - 3)
                 if live(i + 2):
                     quantise_pixels(i + 2)
                 if live(i - 2):
                     scale_maxima(i - 2)
-                if live(i - 3):
-                    normalise_on_vector(i - 3)
-                if live(i):
-                    interleave_query_on_scalar(i)
-                if live(i - 3):
-                    normalise_on_scalar(i - 3)
-                if live(i + 1) and i > 0 and chunks[i + 1][1] == 0:
-                    interleave_keys(chunks[i + 1][0])
+                if live(i - 4):
+                    normalise_on_vector(i - 4)
                 if live(i) and i > 0 and chunks[i][1] == 0:
                     quantise_keys(chunks[i][0])
+                if live(i):
+                    interleave_query_on_scalar(i)
+                if live(i - 4):
+                    normalise_on_scalar(i - 4)
+                if live(i + 1) and i > 0 and chunks[i + 1][1] == 0:
+                    interleave_keys(chunks[i + 1][0])

@@ -22,6 +22,7 @@ CHUNK = 512
 LAST_IMAGE_WIDTHS = (512, 256, 256)
 SCALAR_SHARE = 144
 VECTOR_TILES = 3
+WARM_UP = 6
 RUN = 4
 SIM_SCALE = 1.0 / math.sqrt(CHANNELS)
 
@@ -62,6 +63,8 @@ def tile_spatialocr_module_pa_kernel(tc, h_pix, wp2, sp2, bp2, key_obj, out):
 
         zero = once.tile([P, 1], F32)
         one = once.tile([P, 1], F32)
+        blank = once.tile([P, CHUNK], BF16)
+        nc.vector.memset(blank[:], 0.0)
         nc.vector.memset(zero[:], 0.0)
         nc.scalar.activation(out=one[:], in_=zero[:], func=ACT.Exp)
 
@@ -73,30 +76,33 @@ def tile_spatialocr_module_pa_kernel(tc, h_pix, wp2, sp2, bp2, key_obj, out):
         h_raw, w_raw, key_raw = {}, {}, {}
 
         def pieces(c):
-            return 2 if c == 0 else 1
+            return 2 if c == 1 else 1
 
-        def load_pixels(c):
+        def load_pixels(c, half=0):
             n, first, width = chunks[c]
-            h_raw[c] = raw.tile([P, PACK, width], BF16, name="h_raw")
+            if half == 0:
+                h_raw[c] = raw.tile([P, PACK, width], BF16, name="h_raw")
             piece = width // pieces(c)
-            for lo in range(0, width, piece):
-                nc.sync.dma_start(
-                    out=h_raw[c][:, :, lo : lo + piece],
-                    in_=h_pix[n, :, first + lo : first + lo + piece].rearrange(
-                        "(p t) w -> p t w", t=PACK
-                    ),
-                )
+            lo = half * piece
+            nc.sync.dma_start(
+                out=h_raw[c][:, :, lo : lo + piece],
+                in_=h_pix[n, :, first + lo : first + lo + piece].rearrange(
+                    "(p t) w -> p t w", t=PACK
+                ),
+            )
 
         def load_keys(n):
             key_raw[n] = blocks.tile([P, PACK, REGIONS], BF16, name="key_raw")
             nc.sync.dma_start(out=key_raw[n][:], in_=key_obj[n].rearrange("(p t) r -> p t r", t=PACK))
 
         load_pixels(0)
+        load_pixels(1, 0)
         for t in range(PACK):
             w_raw[t] = blocks.tile([P, CHANNELS], BF16, name="w_raw")
             nc.sync.dma_start(out=w_raw[t][:], in_=wp2.rearrange("(m t) k -> t m k", t=PACK)[t])
+        load_pixels(1, 1)
         load_keys(0)
-        for c in range(1, CHUNKS):
+        for c in range(2, CHUNKS):
             load_pixels(c)
             if chunks[c][1] == 0:
                 load_keys(chunks[c][0])
@@ -259,20 +265,24 @@ def tile_spatialocr_module_pa_kernel(tc, h_pix, wp2, sp2, bp2, key_obj, out):
         w_codes = once.tile([P, PACK * P], U32, align_bytes=64)
         w_scales = once.tile([P, PACK * P], U8, align_bytes=64)
 
-        def prepare_weights():
-            for t in range(PACK):
-                w_words = w_raw[t][:].bitcast(F32).rearrange("m (p u) -> m u p", u=2)
-                w_t = psum_y.tile([P, 2, P], F32, tag="y")
-                for u in range(2):
-                    nc.tensor.transpose(w_t[:, u, :], w_words[:, u, :], identity[:])
-                w_grouped = blocks.tile([P, P, PACK], BF16, name="w_grouped", align_bytes=64)
-                nc.scalar.copy(
-                    out=w_grouped[:].rearrange("p m t -> p (m t)").bitcast(F32).rearrange(
-                        "p (m u) -> p m u", u=2
-                    ),
-                    in_=w_t[:].rearrange("p u m -> p m u"),
-                )
-                quantise(w_grouped[:], w_codes[:, t * P : (t + 1) * P], w_scales[:, t * P : (t + 1) * P])
+        def prepare_weights(t):
+            w_words = w_raw[t][:].bitcast(F32).rearrange("m (p u) -> m u p", u=2)
+            w_t = psum_y.tile([P, 2, P], F32, tag="y")
+            for u in range(2):
+                nc.tensor.transpose(w_t[:, u, :], w_words[:, u, :], identity[:])
+            w_grouped = blocks.tile([P, P, PACK], BF16, name="w_grouped", align_bytes=64)
+            nc.scalar.copy(
+                out=w_grouped[:].rearrange("p m t -> p (m t)").bitcast(F32).rearrange(
+                    "p (m u) -> p m u", u=2
+                ),
+                in_=w_t[:].rearrange("p u m -> p m u"),
+            )
+            quantise(w_grouped[:], w_codes[:, t * P : (t + 1) * P], w_scales[:, t * P : (t + 1) * P])
+
+        def warm_up():
+            unread = psum_y.tile([P, CHUNK], F32, tag="y")
+            for k in range(WARM_UP):
+                nc.tensor.matmul(out=unread[:], lhsT=blank[:, :P], rhs=blank[:], start=True, stop=True)
 
         def live(c):
             return 0 <= c < CHUNKS
@@ -280,13 +290,17 @@ def tile_spatialocr_module_pa_kernel(tc, h_pix, wp2, sp2, bp2, key_obj, out):
         with tc.manual_schedule(
             engines={mybir.EngineType.Activation, mybir.EngineType.DVE, mybir.EngineType.PE}
         ):
-            interleave_pixels(0, 0)
-            interleave_pixels(0, 1)
+            warm_up()
+            whole_pixels(0)
             quantise_pixels(0)
-            prepare_weights()
+            interleave_pixels(1, 0)
+            prepare_weights(0)
+            prepare_weights(1)
+            interleave_pixels(1, 1)
+            prepare_weights(2)
+            prepare_weights(3)
             interleave_keys(0)
             project(0)
-            whole_pixels(1)
             quantise_keys(0)
             quantise_pixels(1)
             for i in range(CHUNKS + 4):

@@ -20,7 +20,7 @@ PIXELS = 1024
 REGIONS = 128
 CHUNK = 512
 LAST_IMAGE_WIDTHS = (512, 256, 256)
-SCALAR_SHARE = 144
+SCALAR_SHARE = 80
 VECTOR_TILES = 3
 WARM_UP = 6
 RUN = 4

@@ -20,7 +20,7 @@ PIXELS = 1024
 REGIONS = 128
 CHUNK = 512
 LAST_IMAGE_WIDTHS = (512, 256, 256)
-SCALAR_SHARE = 80
+SCALAR_SHARE = 112
 VECTOR_TILES = 3
 WARM_UP = 6
 RUN = 4
@@ -158,8 +158,8 @@ def tile_spatialocr_module_pa_kernel(tc, h_pix, wp2, sp2, bp2, key_obj, out):
             q_planes[c] = work.tile([P, PACK, chunks[c][2]], BF16, name="q_planes")
             for t in range(PACK):
                 nc.scalar.activation(
-                    out=q_planes[c][:, t, :],
-                    in_=y_banks[c][t][:],
+                    out=q_planes[c][:, t, :].rearrange("p (g m) -> p g m", m=P),
+                    in_=y_banks[c][t][:].rearrange("p (m g) -> p g m", m=P),
                     func=ACT.Relu,
                     bias=shift[:, t : t + 1],
                     scale=gain[:, t : t + 1],
@@ -245,7 +245,6 @@ def tile_spatialocr_module_pa_kernel(tc, h_pix, wp2, sp2, bp2, key_obj, out):
                 nc.vector.tensor_scalar_mul(
                     out=prob[c][:, g, :], in0=prob[c][:, g, :], scalar1=inverse[c][:, g : g + 1]
                 )
-                store(c, g)
 
         def normalise_on_scalar(c):
             for g in range(chunks[c][2] // P - VECTOR_TILES):
@@ -255,12 +254,12 @@ def tile_spatialocr_module_pa_kernel(tc, h_pix, wp2, sp2, bp2, key_obj, out):
                     func=ACT.Copy,
                     scale=inverse[c][:, g : g + 1],
                 )
-                store(c, g)
 
-        def store(c, g):
+        def store(c):
             n, start, width = chunks[c]
-            first = start + g * P
-            nc.sync.dma_start(out=out[n, first : first + P, :], in_=prob[c][:, g, :])
+            nc.sync.dma_start(
+                out=out[n, start : start + width, :].rearrange("(m g) r -> m g r", m=P), in_=prob[c][:]
+            )
 
         w_codes = once.tile([P, PACK * P], U32, align_bytes=64)
         w_scales = once.tile([P, PACK * P], U8, align_bytes=64)
@@ -333,5 +332,6 @@ def tile_spatialocr_module_pa_kernel(tc, h_pix, wp2, sp2, bp2, key_obj, out):
                     interleave_query_on_scalar(i)
                 if live(i - 4):
                     normalise_on_scalar(i - 4)
+                    store(i - 4)
                 if live(i + 1) and i > 0 and chunks[i + 1][1] == 0:
                     interleave_keys(chunks[i + 1][0])

@@ -43,8 +43,8 @@ def tile_spatialocr_module_pa_kernel(tc, h_pix, wp2, sp2, bp2, key_obj, out):
         CHUNKS = len(chunks)
         raw = ctx.enter_context(tc.tile_pool(name="raw", bufs=CHUNKS))
         blocks = ctx.enter_context(tc.tile_pool(name="blocks", bufs=PACK))
-        work = ctx.enter_context(tc.tile_pool(name="work", bufs=4))
-        small = ctx.enter_context(tc.tile_pool(name="small", bufs=8))
+        work = ctx.enter_context(tc.tile_pool(name="work", bufs=6))
+        small = ctx.enter_context(tc.tile_pool(name="small", bufs=10))
         psum_y = ctx.enter_context(tc.psum_pool(name="psum_y", bufs=6))
         psum_sim = ctx.enter_context(tc.psum_pool(name="psum_sim", bufs=2))
 
@@ -221,10 +221,22 @@ def tile_spatialocr_module_pa_kernel(tc, h_pix, wp2, sp2, bp2, key_obj, out):
                 op1=ALU.add,
             )
 
+        def paired(c):
+            return chunks[c][0] < IMAGES - 1
+
+        def normalised_with(c):
+            if not paired(c):
+                return [c]
+            return [c - 1, c] if c % 2 == 1 else []
+
         def exponentials(c):
             tiles = chunks[c][2] // P
-            prob[c] = work.tile([P, tiles, REGIONS], F32, name="prob", bufs=4)
-            row_sum[c] = small.tile([P, tiles], F32, name="row_sum")
+            prob[c] = work.tile([P, tiles, REGIONS], F32, name="prob", bufs=8)
+            if paired(c) and c % 2 == 1:
+                row_sum[c] = row_sum[c - 1]
+            else:
+                row_sum[c] = small.tile([P, (2 if paired(c) else 1) * tiles], F32, name="row_sum")
+            first = tiles if paired(c) and c % 2 == 1 else 0
             for g in range(tiles):
                 nc.scalar.activation(
                     out=prob[c][:, g, :],
@@ -232,12 +244,19 @@ def tile_spatialocr_module_pa_kernel(tc, h_pix, wp2, sp2, bp2, key_obj, out):
                     func=ACT.Exp,
                     bias=shift_exp[c][:, g : g + 1],
                     scale=SIM_SCALE,
-                    accum_out=row_sum[c][:, g : g + 1],
+                    accum_out=row_sum[c][:, first + g : first + g + 1],
                 )
 
         def invert_sums(c):
-            inverse[c] = small.tile([P, chunks[c][2] // P], F32, name="inverse")
-            nc.vector.reciprocal(out=inverse[c][:], in_=row_sum[c][:])
+            sums = row_sum[c]
+            both = small.tile(list(sums.shape), F32, name="inverse")
+            nc.vector.reciprocal(out=both[:], in_=sums[:])
+            tiles = chunks[c][2] // P
+            if paired(c):
+                inverse[c - 1] = both[:, :tiles]
+                inverse[c] = both[:, tiles:]
+            else:
+                inverse[c] = both[:]
 
         def normalise_on_vector(c):
             tiles = chunks[c][2] // P
@@ -316,7 +335,7 @@ def tile_spatialocr_module_pa_kernel(tc, h_pix, wp2, sp2, bp2, key_obj, out):
                 if live(i - 1):
                     quantise_query(i - 1)
                     attend(i - 1)
-                if live(i - 4):
+                if live(i - 4) and normalised_with(i - 4):
                     invert_sums(i - 4)
                 if live(i - 2):
                     row_maxima(i - 2)
@@ -325,13 +344,15 @@ def tile_spatialocr_module_pa_kernel(tc, h_pix, wp2, sp2, bp2, key_obj, out):
                 if live(i - 2):
                     scale_maxima(i - 2)
                 if live(i - 4):
-                    normalise_on_vector(i - 4)
+                    for c in normalised_with(i - 4):
+                        normalise_on_vector(c)
                 if live(i) and i > 0 and chunks[i][1] == 0:
                     quantise_keys(chunks[i][0])
                 if live(i):
                     interleave_query_on_scalar(i)
                 if live(i - 4):
-                    normalise_on_scalar(i - 4)
-                    store(i - 4)
+                    for c in normalised_with(i - 4):
+                        normalise_on_scalar(c)
+                        store(c)
                 if live(i + 1) and i > 0 and chunks[i + 1][1] == 0:
                     interleave_keys(chunks[i + 1][0])

import math
from contextlib import ExitStack

import concourse.mybir as mybir
from concourse.masks import make_identity

F32 = mybir.dt.float32
BF16 = mybir.dt.bfloat16
U32 = mybir.dt.uint32
U8 = mybir.dt.uint8
FP8X4 = mybir.dt.float8_e4m3fn_x4
ACT = mybir.ActivationFunctionType
ALU = mybir.AluOpType

P = 128
PACK = 4
IMAGES = 4
CHANNELS = P * PACK
PIXELS = 1024
REGIONS = 128
CHUNK = 512
LAST_IMAGE_WIDTHS = (512, 256, 256)
SCALAR_SHARE = 112
VECTOR_TILES = 3
WARM_UP = 6
RUN = 4
SIM_SCALE = 1.0 / math.sqrt(CHANNELS)

FLOPS = 2 * IMAGES * PIXELS * CHANNELS * (CHANNELS + REGIONS)


def tile_spatialocr_module_pa_kernel(tc, h_pix, wp2, sp2, bp2, key_obj, out):
    nc = tc.nc
    with ExitStack() as ctx:
        once = ctx.enter_context(tc.tile_pool(name="once", bufs=1))
        chunks = []
        for n in range(IMAGES):
            widths = LAST_IMAGE_WIDTHS if n == IMAGES - 1 else (CHUNK,) * (PIXELS // CHUNK)
            first = 0
            for width in widths:
                chunks.append((n, first, width))
                first += width
        CHUNKS = len(chunks)
        raw = ctx.enter_context(tc.tile_pool(name="raw", bufs=CHUNKS))
        blocks = ctx.enter_context(tc.tile_pool(name="blocks", bufs=PACK))
        work = ctx.enter_context(tc.tile_pool(name="work", bufs=6))
        small = ctx.enter_context(tc.tile_pool(name="small", bufs=10))
        psum_y = ctx.enter_context(tc.psum_pool(name="psum_y", bufs=6))
        psum_sim = ctx.enter_context(tc.psum_pool(name="psum_sim", bufs=2))

        def interleave(copy, grouped, planes):
            copy(
                out=grouped.rearrange("p (c i) t -> p c t i", i=RUN),
                in_=planes.rearrange("p t (c i) -> p c t i", i=RUN),
            )

        def quantise(grouped, codes, scales):
            nc.vector.quantize_mx(
                out=codes.bitcast(FP8X4),
                scales=scales,
                in_=grouped.rearrange("p w t -> p (w t)"),
            )

        zero = once.tile([P, 1], F32)
        one = once.tile([P, 1], F32)
        blank = once.tile([P, CHUNK], BF16)
        nc.vector.memset(blank[:], 0.0)
        nc.vector.memset(zero[:], 0.0)
        nc.scalar.activation(out=one[:], in_=zero[:], func=ACT.Exp)

        gain_bf = once.tile([P, PACK], BF16)
        shift_bf = once.tile([P, PACK], BF16)
        nc.scalar.dma_start(out=gain_bf[:], in_=sp2.rearrange("(p t) -> p t", t=PACK))
        nc.scalar.dma_start(out=shift_bf[:], in_=bp2.rearrange("(p t) -> p t", t=PACK))

        h_raw, w_raw, key_raw = {}, {}, {}

        def pieces(c):
            return 2 if c == 1 else 1

        def load_pixels(c, half=0):
            n, first, width = chunks[c]
            if half == 0:
                h_raw[c] = raw.tile([P, PACK, width], BF16, name="h_raw")
            piece = width // pieces(c)
            lo = half * piece
            nc.sync.dma_start(
                out=h_raw[c][:, :, lo : lo + piece],
                in_=h_pix[n, :, first + lo : first + lo + piece].rearrange(
                    "(p t) w -> p t w", t=PACK
                ),
            )

        def load_keys(n):
            key_raw[n] = blocks.tile([P, PACK, REGIONS], BF16, name="key_raw")
            nc.sync.dma_start(out=key_raw[n][:], in_=key_obj[n].rearrange("(p t) r -> p t r", t=PACK))

        load_pixels(0)
        load_pixels(1, 0)
        for t in range(PACK):
            w_raw[t] = blocks.tile([P, CHANNELS], BF16, name="w_raw")
            nc.sync.dma_start(out=w_raw[t][:], in_=wp2.rearrange("(m t) k -> t m k", t=PACK)[t])
        load_pixels(1, 1)
        load_keys(0)
        for c in range(2, CHUNKS):
            load_pixels(c)
            if chunks[c][1] == 0:
                load_keys(chunks[c][0])

        identity = once.tile([P, P], F32)
        make_identity(nc, identity[:])
        gain = once.tile([P, PACK], F32)
        shift = once.tile([P, PACK], F32)
        nc.gpsimd.tensor_copy(out=gain[:], in_=gain_bf[:])
        nc.gpsimd.tensor_copy(out=shift[:], in_=shift_bf[:])

        h_grouped, h_codes, h_scales = {}, {}, {}
        q_planes, q_grouped, q_codes, q_scales = {}, {}, {}, {}
        key_grouped, key_codes, key_scales = {}, {}, {}
        y_banks, sim, row_max, shift_exp, row_sum, inverse, prob = {}, {}, {}, {}, {}, {}, {}

        def interleave_pixels(c, half):
            if half == 0:
                h_grouped[c] = work.tile([P, chunks[c][2], PACK], BF16, name="h_grouped", align_bytes=64)
            piece = chunks[c][2] // 2
            lo = half * piece
            interleave(
                nc.vector.tensor_copy,
                h_grouped[c][:, lo : lo + piece, :],
                h_raw[c][:, :, lo : lo + piece],
            )

        def whole_pixels(c):
            h_grouped[c] = work.tile([P, chunks[c][2], PACK], BF16, name="h_grouped", align_bytes=64)
            interleave(nc.vector.tensor_copy, h_grouped[c][:], h_raw[c][:])

        def quantise_pixels(c):
            h_codes[c] = work.tile([P, chunks[c][2]], U32, name="h_codes", align_bytes=64)
            h_scales[c] = work.tile([P, chunks[c][2]], U8, name="h_scales", align_bytes=64)
            quantise(h_grouped[c][:], h_codes[c][:], h_scales[c][:])

        def project(c):
            y_banks[c] = []
            for t in range(PACK):
                y = psum_y.tile([P, chunks[c][2]], F32, tag="y")
                y_banks[c].append(y)
                nc.tensor.matmul_mx(
                    out=y[:],
                    lhsT=w_codes[:, t * P : (t + 1) * P].bitcast(FP8X4),
                    lhsT_scale=w_scales[:, t * P : (t + 1) * P],
                    rhs=h_codes[c][:].bitcast(FP8X4),
                    rhs_scale=h_scales[c][:],
                    start=True,
                    stop=True,
                )

        def rectify(c):
            q_planes[c] = work.tile([P, PACK, chunks[c][2]], BF16, name="q_planes")
            for t in range(PACK):
                nc.scalar.activation(
                    out=q_planes[c][:, t, :].rearrange("p (g m) -> p g m", m=P),
                    in_=y_banks[c][t][:].rearrange("p (m g) -> p g m", m=P),
                    func=ACT.Relu,
                    bias=shift[:, t : t + 1],
                    scale=gain[:, t : t + 1],
                )

        def interleave_keys(n):
            key_grouped[n] = blocks.tile([P, REGIONS, PACK], BF16, name="key_grouped", align_bytes=64)
            interleave(nc.scalar.copy, key_grouped[n][:], key_raw[n][:])

        def quantise_keys(n):
            key_codes[n] = blocks.tile([P, REGIONS], U32, name="key_codes", align_bytes=64)
            key_scales[n] = blocks.tile([P, REGIONS], U8, name="key_scales", align_bytes=64)
            quantise(key_grouped[n][:], key_codes[n][:], key_scales[n][:])

        def vector_share(c):
            return chunks[c][2] - (SCALAR_SHARE if chunks[c][2] == CHUNK else 0)

        def interleave_query_on_scalar(c):
            q_grouped[c] = work.tile([P, chunks[c][2], PACK], BF16, name="q_grouped", align_bytes=64)
            mine = vector_share(c)
            if mine < chunks[c][2]:
                interleave(nc.scalar.copy, q_grouped[c][:, mine:, :], q_planes[c][:, :, mine:])

        def interleave_query_on_vector(c):
            mine = vector_share(c)
            interleave(nc.vector.tensor_copy, q_grouped[c][:, :mine, :], q_planes[c][:, :, :mine])

        def quantise_query(c):
            q_codes[c] = work.tile([P, chunks[c][2]], U32, name="q_codes", align_bytes=64)
            q_scales[c] = work.tile([P, chunks[c][2]], U8, name="q_scales", align_bytes=64)
            quantise(q_grouped[c][:], q_codes[c][:], q_scales[c][:])

        def attend(c):
            n = chunks[c][0]
            sim[c] = psum_sim.tile([P, chunks[c][2] // P, REGIONS], F32, name="sim")
            for g in range(chunks[c][2] // P):
                nc.tensor.matmul_mx(
                    out=sim[c][:, g, :],
                    lhsT=q_codes[c][:, g * P : (g + 1) * P].bitcast(FP8X4),
                    lhsT_scale=q_scales[c][:, g * P : (g + 1) * P],
                    rhs=key_codes[n][:].bitcast(FP8X4),
                    rhs_scale=key_scales[n][:],
                    start=True,
                    stop=True,
                )

        def row_maxima(c):
            row_max[c] = small.tile([P, chunks[c][2] // P], F32, name="row_max")
            nc.vector.tensor_reduce(out=row_max[c][:], in_=sim[c][:], axis=mybir.AxisListType.X, op=ALU.max)

        def scale_maxima(c):
            shift_exp[c] = small.tile([P, chunks[c][2] // P], F32, name="shift_exp")
            nc.gpsimd.tensor_scalar(
                out=shift_exp[c][:],
                in0=row_max[c][:],
                scalar1=-SIM_SCALE,
                scalar2=0.0,
                op0=ALU.mult,
                op1=ALU.add,
            )

        def paired(c):
            return chunks[c][0] < IMAGES - 1

        def normalised_with(c):
            if not paired(c):
                return [c]
            return [c - 1, c] if c % 2 == 1 else []

        def exponentials(c):
            tiles = chunks[c][2] // P
            prob[c] = work.tile([P, tiles, REGIONS], F32, name="prob", bufs=8)
            if paired(c) and c % 2 == 1:
                row_sum[c] = row_sum[c - 1]
            else:
                row_sum[c] = small.tile([P, (2 if paired(c) else 1) * tiles], F32, name="row_sum")
            first = tiles if paired(c) and c % 2 == 1 else 0
            for g in range(tiles):
                nc.scalar.activation(
                    out=prob[c][:, g, :],
                    in_=sim[c][:, g, :],
                    func=ACT.Exp,
                    bias=shift_exp[c][:, g : g + 1],
                    scale=SIM_SCALE,
                    accum_out=row_sum[c][:, first + g : first + g + 1],
                )

        def invert_sums(c):
            sums = row_sum[c]
            both = small.tile(list(sums.shape), F32, name="inverse")
            nc.vector.reciprocal(out=both[:], in_=sums[:])
            tiles = chunks[c][2] // P
            if paired(c):
                inverse[c - 1] = both[:, :tiles]
                inverse[c] = both[:, tiles:]
            else:
                inverse[c] = both[:]

        def normalise_on_vector(c):
            tiles = chunks[c][2] // P
            for g in range(max(0, tiles - VECTOR_TILES), tiles):
                nc.vector.tensor_scalar_mul(
                    out=prob[c][:, g, :], in0=prob[c][:, g, :], scalar1=inverse[c][:, g : g + 1]
                )

        def normalise_on_scalar(c):
            for g in range(chunks[c][2] // P - VECTOR_TILES):
                nc.scalar.activation(
                    out=prob[c][:, g, :],
                    in_=prob[c][:, g, :],
                    func=ACT.Copy,
                    scale=inverse[c][:, g : g + 1],
                )

        def store(c):
            n, start, width = chunks[c]
            nc.sync.dma_start(
                out=out[n, start : start + width, :].rearrange("(m g) r -> m g r", m=P), in_=prob[c][:]
            )

        w_codes = once.tile([P, PACK * P], U32, align_bytes=64)
        w_scales = once.tile([P, PACK * P], U8, align_bytes=64)

        def prepare_weights(t):
            w_words = w_raw[t][:].bitcast(F32).rearrange("m (p u) -> m u p", u=2)
            w_t = psum_y.tile([P, 2, P], F32, tag="y")
            for u in range(2):
                nc.tensor.transpose(w_t[:, u, :], w_words[:, u, :], identity[:])
            w_grouped = blocks.tile([P, P, PACK], BF16, name="w_grouped", align_bytes=64)
            nc.scalar.copy(
                out=w_grouped[:].rearrange("p m t -> p (m t)").bitcast(F32).rearrange(
                    "p (m u) -> p m u", u=2
                ),
                in_=w_t[:].rearrange("p u m -> p m u"),
            )
            quantise(w_grouped[:], w_codes[:, t * P : (t + 1) * P], w_scales[:, t * P : (t + 1) * P])

        def warm_up():
            unread = psum_y.tile([P, CHUNK], F32, tag="y")
            for k in range(WARM_UP):
                nc.tensor.matmul(out=unread[:], lhsT=blank[:, :P], rhs=blank[:], start=True, stop=True)

        def live(c):
            return 0 <= c < CHUNKS

        with tc.manual_schedule(
            engines={mybir.EngineType.Activation, mybir.EngineType.DVE, mybir.EngineType.PE}
        ):
            warm_up()
            whole_pixels(0)
            quantise_pixels(0)
            interleave_pixels(1, 0)
            prepare_weights(0)
            prepare_weights(1)
            interleave_pixels(1, 1)
            prepare_weights(2)
            prepare_weights(3)
            interleave_keys(0)
            project(0)
            quantise_keys(0)
            quantise_pixels(1)
            for i in range(CHUNKS + 4):
                if live(i):
                    rectify(i)
                if live(i - 3):
                    exponentials(i - 3)
                if live(i + 1):
                    project(i + 1)
                if live(i - 1):
                    interleave_query_on_vector(i - 1)
                if live(i + 2):
                    whole_pixels(i + 2)
                if live(i - 1):
                    quantise_query(i - 1)
                    attend(i - 1)
                if live(i - 4) and normalised_with(i - 4):
                    invert_sums(i - 4)
                if live(i - 2):
                    row_maxima(i - 2)
                if live(i + 2):
                    quantise_pixels(i + 2)
                if live(i - 2):
                    scale_maxima(i - 2)
                if live(i - 4):
                    for c in normalised_with(i - 4):
                        normalise_on_vector(c)
                if live(i) and i > 0 and chunks[i][1] == 0:
                    quantise_keys(chunks[i][0])
                if live(i):
                    interleave_query_on_scalar(i)
                if live(i - 4):
                    for c in normalised_with(i - 4):
                        normalise_on_scalar(c)
                        store(c)
                if live(i + 1) and i > 0 and chunks[i + 1][1] == 0:
                    interleave_keys(chunks[i + 1][0])
